import numpy as np
import ml_dtypes


def mxq(x, axis, fmt="e4m3"):
    dtype, down = {"e4m3": (ml_dtypes.float8_e4m3fn, 7), "e5m2": (ml_dtypes.float8_e5m2, 14)}[fmt]
    v = np.moveaxis(np.asarray(x, np.float32).astype(ml_dtypes.bfloat16).astype(np.float64), axis, -1)
    blocks = v.reshape(v.shape[:-1] + (-1, 32))
    amax = np.abs(blocks).max(-1, keepdims=True)
    byte = np.maximum(np.where(amax > 0, np.frexp(amax)[1] - 1 + 127, 0) - down, 1)
    scale = np.exp2(byte - 127.0)
    codes = (blocks / scale).astype(np.float32).astype(dtype).astype(np.float64)
    return np.moveaxis((codes * scale).reshape(v.shape), -1, axis)


WIDE = False


def mx_kscale(k):
    if not WIDE:
        return np.ones(k)
    levels = np.array([10, -10, 5, -5, 0])
    a = np.random.permutation(np.resize(levels, k // 512 * 4)).reshape(k // 512, 4)
    idx = np.arange(k)
    return np.exp2(a[idx // 512, idx % 128 // 32])


BF16 = ml_dtypes.bfloat16


def bf(x):
    return np.asarray(x, np.float32).astype(BF16)


def f64(x):
    return np.asarray(x).astype(np.float64)


B, N, F, D, DIM = 8, 1024, 1024, 512, 32
EPS = 1e-6
RAD = 3.0


def expmap0_full(us):
    r = np.sqrt((us * us).sum(-1, keepdims=True))
    rs = np.maximum(r, EPS)
    x0 = 0.5 * (np.exp(r) + np.exp(-r))
    xs = (0.5 * (np.exp(rs) - np.exp(-rs)) / rs) * us
    return np.concatenate([x0, xs], axis=-1)


def setup_inputs():
    s = mx_kscale(F)
    amp = 0.5 + 0.5 * np.random.random((B, N, 1))
    return {"x": bf(np.random.standard_normal((B, N, F)) * amp * s),
            "w_sp": bf(np.random.standard_normal((F, D)) * RAD / np.sqrt(D * F) / s[:, None])}


def reference(x, w_sp):
    us = mxq(f64(x), 2, "e4m3") @ mxq(f64(w_sp), 0, "e4m3")
    return expmap0_full(us)

@@ -1,0 +1,229 @@
+import concourse.mybir as mybir
+from concourse.masks import make_identity
+
+BF16 = mybir.dt.bfloat16
+F32 = mybir.dt.float32
+U32 = mybir.dt.uint32
+U8 = mybir.dt.uint8
+FP8X4 = mybir.dt.float8_e4m3fn_x4
+ACT = mybir.ActivationFunctionType
+ALU = mybir.AluOpType
+
+P = 128
+GRAPHS, NODES, FEATURES, DIMS = 8, 1024, 1024, 512
+PACK = 4
+K_PASS = P * PACK
+PASSES = FEATURES // K_PASS
+HALVES = 2
+TILES = NODES // P
+PAIR = 2
+PAIRS = TILES // PAIR
+N_PAIRS = GRAPHS * PAIRS
+TILE_COLS = PASSES * P * PACK
+TILE_WORDS = PASSES * P
+OUT_COLS = 1 + DIMS
+RUN = 4
+EPS = 1e-6
+TWO_SINH_EPS = 2.0 * EPS * (1.0 + EPS * EPS / 6.0)
+PIECE = 1024
+PAIRS_IN_PSUM = 3
+VECTOR_COPIES_EVERY = 3
+
+MULTIPLY_AT = 2
+EXP_AT = 3
+SCALE_AT = 4
+STORE_AT = 5
+
+FLOPS = 2 * GRAPHS * NODES * FEATURES * DIMS
+
+
+def tile_hgcn_pb_t_kernel(tc, x, w_sp, out):
+    nc = tc.nc
+    with (
+        tc.tile_pool(name="const", bufs=1) as const,
+        tc.tile_pool(name="x_pool", bufs=GRAPHS) as x_pool,
+        tc.tile_pool(name="out_pool", bufs=3) as out_pool,
+        tc.tile_pool(name="mx_pool", bufs=MULTIPLY_AT + 2) as mx_pool,
+        tc.tile_pool(name="small", bufs=4) as small,
+        tc.psum_pool(name="xt_pool", bufs=PAIR) as xt_pool,
+        tc.psum_pool(name="us_pool", bufs=PAIRS_IN_PSUM * PAIR) as us_pool,
+        tc.manual_schedule(),
+    ):
+        x_sb, out_sb = {}, {}
+        x_t, grouped, codes, scales, us = {}, {}, {}, {}, {}
+        sumsq, radius, clamped, e_pos, e_neg, inverse, diff, sinh = {}, {}, {}, {}, {}, {}, {}, {}
+
+        def load_nodes(b, first_tile, n_tiles):
+            rows = x[b].rearrange("(p j) k -> p j k", j=TILES)
+            cut = slice(first_tile, first_tile + n_tiles)
+            nc.sync.dma_start(out=x_sb[b][:, cut, :], in_=rows[:, cut, :])
+
+        for b in range(GRAPHS):
+            x_sb[b] = x_pool.tile([P, TILES, FEATURES], BF16, name="x_sb")
+
+        load_nodes(0, 0, 1)
+        w_raw = const.tile([P, PASSES, PACK, DIMS], BF16)
+        w_rows = w_sp.rearrange("(g u p e) d -> g p u (e d)", g=PASSES, u=HALVES, p=P)
+        for g in range(PASSES):
+            nc.sync.dma_start(out=w_raw[:, g].rearrange("p (u e) d -> p u (e d)", u=HALVES), in_=w_rows[g])
+        load_nodes(0, 1, 1)
+        for q in range(1, PAIRS):
+            load_nodes(0, PAIR * q, PAIR)
+        for b in range(1, GRAPHS):
+            load_nodes(b, 0, TILES)
+
+        ident = const.tile([P, P], F32)
+        make_identity(nc, ident[:])
+        half = const.tile([P, PAIR], F32)
+        nc.gpsimd.memset(half[:], 0.5)
+
+        w_grouped = const.tile([P, PASSES, DIMS, PACK], BF16, align_bytes=64)
+        for g in range(PASSES):
+            nc.vector.tensor_copy(
+                out=w_grouped[:, g].rearrange("p (c i) t -> p c t i", i=RUN),
+                in_=w_raw[:, g].rearrange("p t (c i) -> p c t i", i=RUN),
+            )
+        w_codes = const.tile([P, PASSES * DIMS], U32, align_bytes=64)
+        w_scales = const.tile([P, PASSES * DIMS], U8, align_bytes=64)
+        nc.vector.quantize_mx(
+            out=w_codes[:].bitcast(FP8X4),
+            scales=w_scales[:],
+            in_=w_grouped[:].rearrange("p g d t -> p (g d t)"),
+        )
+
+        def transpose_pair(n):
+            b, q = divmod(n, PAIRS)
+            for i in range(PAIR):
+                words = x_sb[b][:, PAIR * q + i, :].bitcast(F32)
+                bank = xt_pool.tile([P, PASSES, HALVES, P], F32, name="x_t")
+                for g in range(PASSES):
+                    for u in range(HALVES):
+                        first = (g * HALVES + u) * P
+                        nc.tensor.transpose(bank[:, g, u, :], words[:, first : first + P], ident[:])
+                x_t[n, i] = bank
+
+        def copy_out_pair(n):
+            grouped[n] = mx_pool.tile([P, PAIR * TILE_COLS], BF16, align_bytes=64, name="grouped")
+            for i in range(PAIR):
+                dst = grouped[n][:, i * TILE_COLS : (i + 1) * TILE_COLS].bitcast(F32)
+                dst = dst.rearrange("p (g r u) -> p g r u", g=PASSES, u=HALVES)
+                src = x_t[n, i][:].rearrange("p g u r -> p g r u")
+                if i == PAIR - 1 and n % VECTOR_COPIES_EVERY == VECTOR_COPIES_EVERY - 1:
+                    nc.vector.tensor_copy(out=dst, in_=src)
+                else:
+                    nc.scalar.copy(out=dst, in_=src)
+
+        def quantise_pair(n):
+            codes[n] = mx_pool.tile([P, PAIR * TILE_WORDS], U32, align_bytes=64, name="codes")
+            scales[n] = mx_pool.tile([P, PAIR * TILE_WORDS], U8, align_bytes=64, name="scales")
+            nc.vector.quantize_mx(out=codes[n][:].bitcast(FP8X4), scales=scales[n][:], in_=grouped[n][:])
+
+        def multiply_pair(n):
+            for i in range(PAIR):
+                us[n, i] = us_pool.tile([P, DIMS], F32, name="us")
+                for g in range(PASSES):
+                    nodes = slice((i * PASSES + g) * P, (i * PASSES + g + 1) * P)
+                    dims = slice(g * DIMS, (g + 1) * DIMS)
+                    nc.tensor.matmul_mx(
+                        out=us[n, i][:],
+                        lhsT=codes[n][:, nodes].bitcast(FP8X4),
+                        lhsT_scale=scales[n][:, nodes],
+                        rhs=w_codes[:, dims].bitcast(FP8X4),
+                        rhs_scale=w_scales[:, dims],
+                        start=(g == 0),
+                        stop=(g == PASSES - 1),
+                    )
+
+        def sum_squares(n, i):
+            if i == 0:
+                sumsq[n] = small.tile([P, PAIR], F32, name="sumsq")
+            squares = small.tile([P, DIMS], BF16, name="squares")
+            nc.scalar.activation(out=squares[:], in_=us[n, i][:], func=ACT.Square, accum_out=sumsq[n][:, i : i + 1])
+
+        def take_root(n):
+            radius[n] = small.tile([P, PAIR], F32, name="radius")
+            nc.gpsimd.tensor_tensor(out=radius[n][:], in0=sumsq[n][:], in1=half[:], op=ALU.pow)
+            clamped[n] = small.tile([P, PAIR], F32, name="clamped")
+            nc.gpsimd.tensor_scalar(out=clamped[n][:], in0=radius[n][:], scalar1=EPS, scalar2=None, op0=ALU.max)
+
+        def exponentials(n):
+            e_pos[n] = small.tile([P, PAIR], F32, name="e_pos")
+            e_neg[n] = small.tile([P, PAIR], F32, name="e_neg")
+            nc.scalar.activation(out=e_pos[n][:], in_=radius[n][:], func=ACT.Exp)
+            nc.scalar.activation(out=e_neg[n][:], in_=radius[n][:], func=ACT.Exp, scale=-1.0)
+
+        def invert(n):
+            inverse[n] = small.tile([P, PAIR], F32, name="inverse")
+            nc.vector.reciprocal(out=inverse[n][:], in_=clamped[n][:])
+
+        def subtract(n):
+            diff[n] = small.tile([P, PAIR], F32, name="diff")
+            nc.vector.tensor_sub(out=diff[n][:], in0=e_pos[n][:], in1=e_neg[n][:])
+
+        def sinh_and_cosh(n):
+            b, q = divmod(n, PAIRS)
+            if q == 0:
+                out_sb[b] = out_pool.tile([P, TILES, OUT_COLS], F32, name="out_sb")
+            sinh[n] = small.tile([P, PAIR], F32, name="sinh")
+            nc.vector.tensor_scalar(
+                out=sinh[n][:], in0=diff[n][:], scalar1=TWO_SINH_EPS, scalar2=0.5, op0=ALU.max, op1=ALU.mult
+            )
+            nc.vector.scalar_tensor_tensor(
+                out=out_sb[b][:, PAIR * q : PAIR * (q + 1), 0],
+                in0=diff[n][:],
+                scalar=0.5,
+                in1=e_neg[n][:],
+                op0=ALU.mult,
+                op1=ALU.add,
+            )
+
+        def scale_pair(n):
+            b, q = divmod(n, PAIRS)
+            for i in range(PAIR):
+                nc.vector.tensor_scalar(
+                    out=out_sb[b][:, PAIR * q + i, 1:],
+                    in0=us[n, i][:],
+                    scalar1=inverse[n][:, i : i + 1],
+                    scalar2=sinh[n][:, i : i + 1],
+                    op0=ALU.mult,
+                    op1=ALU.mult,
+                )
+
+        def store_after_pair(n):
+            b, q = divmod(n, PAIRS)
+            last_pair = q == PAIRS - 1
+            if b < GRAPHS - 1 and not last_pair:
+                return
+            first = PIECE * q if b == GRAPHS - 1 else 0
+            end = TILES * OUT_COLS if last_pair else PIECE * (q + 1)
+            nc.scalar.dma_start(
+                out=out[b].rearrange("(p j) d -> p (j d)", j=TILES)[:, first:end],
+                in_=out_sb[b][:].rearrange("p j d -> p (j d)")[:, first:end],
+            )
+
+        def live(n):
+            return 0 <= n < N_PAIRS
+
+        for s in range(N_PAIRS + STORE_AT):
+            if live(s):
+                transpose_pair(s)
+                copy_out_pair(s)
+            if live(s - MULTIPLY_AT):
+                multiply_pair(s - MULTIPLY_AT)
+            if live(s - SCALE_AT):
+                scale_pair(s - SCALE_AT)
+            if live(s - MULTIPLY_AT):
+                sum_squares(s - MULTIPLY_AT, 0)
+            if live(s - STORE_AT):
+                store_after_pair(s - STORE_AT)
+            if live(s - EXP_AT):
+                invert(s - EXP_AT)
+                exponentials(s - EXP_AT)
+                subtract(s - EXP_AT)
+            if live(s - MULTIPLY_AT):
+                sum_squares(s - MULTIPLY_AT, 1)
+                take_root(s - MULTIPLY_AT)
+            if live(s):
+                quantise_pair(s)
+            if live(s - EXP_AT):
+                sinh_and_cosh(s - EXP_AT)

@@ -1,3 +1,5 @@
+import math
+
 import concourse.mybir as mybir
 from concourse.masks import make_identity
 
@@ -23,8 +25,8 @@ TILE_COLS = PASSES * P * PACK
 TILE_WORDS = PASSES * P
 OUT_COLS = 1 + DIMS
 RUN = 4
-EPS = 1e-6
-TWO_SINH_EPS = 2.0 * EPS * (1.0 + EPS * EPS / 6.0)
+LN2 = math.log(2.0)
+NUDGE = 2.0**-50
 PIECE = 1024
 PAIRS_IN_PSUM = 3
 VECTOR_COPIES_EVERY = 3
@@ -51,7 +53,7 @@ def tile_hgcn_pb_t_kernel(tc, x, w_sp, out):
     ):
         x_sb, out_sb = {}, {}
         x_t, grouped, codes, scales, us = {}, {}, {}, {}, {}
-        sumsq, radius, clamped, e_pos, e_neg, inverse, diff, sinh = {}, {}, {}, {}, {}, {}, {}, {}
+        sumsq, radius, e_pos, e_neg, inverse, sinh = {}, {}, {}, {}, {}, {}
 
         def load_nodes(b, first_tile, n_tiles):
             rows = x[b].rearrange("(p j) k -> p j k", j=TILES)
@@ -76,6 +78,11 @@ def tile_hgcn_pb_t_kernel(tc, x, w_sp, out):
         make_identity(nc, ident[:])
         half = const.tile([P, PAIR], F32)
         nc.gpsimd.memset(half[:], 0.5)
+        nudge = const.tile([P, 1], F32)
+        nc.gpsimd.memset(nudge[:], NUDGE)
+        minus_ln2 = const.tile([P, 1], F32)
+        nc.gpsimd.memset(minus_ln2[:], 1.0)
+        nc.vector.tensor_scalar(out=minus_ln2[:], in0=minus_ln2[:], scalar1=-LN2, scalar2=None, op0=ALU.mult)
 
         w_grouped = const.tile([P, PASSES, DIMS, PACK], BF16, align_bytes=64)
         for g in range(PASSES):
@@ -138,44 +145,33 @@ def tile_hgcn_pb_t_kernel(tc, x, w_sp, out):
             if i == 0:
                 sumsq[n] = small.tile([P, PAIR], F32, name="sumsq")
             squares = small.tile([P, DIMS], BF16, name="squares")
-            nc.scalar.activation(out=squares[:], in_=us[n, i][:], func=ACT.Square, accum_out=sumsq[n][:, i : i + 1])
+            nc.scalar.activation(
+                out=squares[:], in_=us[n, i][:], func=ACT.Square, bias=nudge[:], accum_out=sumsq[n][:, i : i + 1]
+            )
 
         def take_root(n):
             radius[n] = small.tile([P, PAIR], F32, name="radius")
             nc.gpsimd.tensor_tensor(out=radius[n][:], in0=sumsq[n][:], in1=half[:], op=ALU.pow)
-            clamped[n] = small.tile([P, PAIR], F32, name="clamped")
-            nc.gpsimd.tensor_scalar(out=clamped[n][:], in0=radius[n][:], scalar1=EPS, scalar2=None, op0=ALU.max)
 
         def exponentials(n):
             e_pos[n] = small.tile([P, PAIR], F32, name="e_pos")
             e_neg[n] = small.tile([P, PAIR], F32, name="e_neg")
-            nc.scalar.activation(out=e_pos[n][:], in_=radius[n][:], func=ACT.Exp)
-            nc.scalar.activation(out=e_neg[n][:], in_=radius[n][:], func=ACT.Exp, scale=-1.0)
+            nc.scalar.activation(out=e_pos[n][:], in_=radius[n][:], func=ACT.Exp, bias=minus_ln2[:])
+            nc.scalar.activation(out=e_neg[n][:], in_=radius[n][:], func=ACT.Exp, bias=minus_ln2[:], scale=-1.0)
 
         def invert(n):
             inverse[n] = small.tile([P, PAIR], F32, name="inverse")
-            nc.vector.reciprocal(out=inverse[n][:], in_=clamped[n][:])
+            nc.vector.reciprocal(out=inverse[n][:], in_=radius[n][:])
 
         def subtract(n):
-            diff[n] = small.tile([P, PAIR], F32, name="diff")
-            nc.vector.tensor_sub(out=diff[n][:], in0=e_pos[n][:], in1=e_neg[n][:])
+            sinh[n] = small.tile([P, PAIR], F32, name="sinh")
+            nc.vector.tensor_sub(out=sinh[n][:], in0=e_pos[n][:], in1=e_neg[n][:])
 
-        def sinh_and_cosh(n):
+        def take_cosh(n):
             b, q = divmod(n, PAIRS)
             if q == 0:
                 out_sb[b] = out_pool.tile([P, TILES, OUT_COLS], F32, name="out_sb")
-            sinh[n] = small.tile([P, PAIR], F32, name="sinh")
-            nc.vector.tensor_scalar(
-                out=sinh[n][:], in0=diff[n][:], scalar1=TWO_SINH_EPS, scalar2=0.5, op0=ALU.max, op1=ALU.mult
-            )
-            nc.vector.scalar_tensor_tensor(
-                out=out_sb[b][:, PAIR * q : PAIR * (q + 1), 0],
-                in0=diff[n][:],
-                scalar=0.5,
-                in1=e_neg[n][:],
-                op0=ALU.mult,
-                op1=ALU.add,
-            )
+            nc.vector.tensor_add(out=out_sb[b][:, PAIR * q : PAIR * (q + 1), 0], in0=e_pos[n][:], in1=e_neg[n][:])
 
         def scale_pair(n):
             b, q = divmod(n, PAIRS)
@@ -226,4 +222,4 @@ def tile_hgcn_pb_t_kernel(tc, x, w_sp, out):
             if live(s):
                 quantise_pair(s)
             if live(s - EXP_AT):
-                sinh_and_cosh(s - EXP_AT)
+                take_cosh(s - EXP_AT)

@@ -29,7 +29,7 @@ LN2 = math.log(2.0)
 NUDGE = 2.0**-50
 PIECE = 1024
 PAIRS_IN_PSUM = 3
-VECTOR_COPIES_EVERY = 3
+VECTOR_COPIES_EVERY = 2
 
 MULTIPLY_AT = 2
 EXP_AT = 3

@@ -63,15 +63,17 @@ def tile_hgcn_pb_t_kernel(tc, x, w_sp, out):
         for b in range(GRAPHS):
             x_sb[b] = x_pool.tile([P, TILES, FEATURES], BF16, name="x_sb")
 
-        load_nodes(0, 0, 1)
         w_raw = const.tile([P, PASSES, PACK, DIMS], BF16)
         w_rows = w_sp.rearrange("(g u p e) d -> g p u (e d)", g=PASSES, u=HALVES, p=P)
         for g in range(PASSES):
             nc.sync.dma_start(out=w_raw[:, g].rearrange("p (u e) d -> p u (e d)", u=HALVES), in_=w_rows[g])
-        load_nodes(0, 1, 1)
+        for j in range(PAIR):
+            load_nodes(0, j, 1)
         for q in range(1, PAIRS):
             load_nodes(0, PAIR * q, PAIR)
-        for b in range(1, GRAPHS):
+        for j in range(0, TILES, TILES // 2):
+            load_nodes(1, j, TILES // 2)
+        for b in range(2, GRAPHS):
             load_nodes(b, 0, TILES)
 
         ident = const.tile([P, P], F32)
@@ -85,18 +87,19 @@ def tile_hgcn_pb_t_kernel(tc, x, w_sp, out):
         nc.vector.tensor_scalar(out=minus_ln2[:], in0=minus_ln2[:], scalar1=-LN2, scalar2=None, op0=ALU.mult)
 
         w_grouped = const.tile([P, PASSES, DIMS, PACK], BF16, align_bytes=64)
+        w_codes = const.tile([P, PASSES * DIMS], U32, align_bytes=64)
+        w_scales = const.tile([P, PASSES * DIMS], U8, align_bytes=64)
         for g in range(PASSES):
             nc.vector.tensor_copy(
                 out=w_grouped[:, g].rearrange("p (c i) t -> p c t i", i=RUN),
                 in_=w_raw[:, g].rearrange("p t (c i) -> p c t i", i=RUN),
             )
-        w_codes = const.tile([P, PASSES * DIMS], U32, align_bytes=64)
-        w_scales = const.tile([P, PASSES * DIMS], U8, align_bytes=64)
-        nc.vector.quantize_mx(
-            out=w_codes[:].bitcast(FP8X4),
-            scales=w_scales[:],
-            in_=w_grouped[:].rearrange("p g d t -> p (g d t)"),
-        )
+            dims = slice(g * DIMS, (g + 1) * DIMS)
+            nc.vector.quantize_mx(
+                out=w_codes[:, dims].bitcast(FP8X4),
+                scales=w_scales[:, dims],
+                in_=w_grouped[:, g].rearrange("p d t -> p (d t)"),
+            )
 
         def transpose_pair(n):
             b, q = divmod(n, PAIRS)
@@ -153,25 +156,38 @@ def tile_hgcn_pb_t_kernel(tc, x, w_sp, out):
             radius[n] = small.tile([P, PAIR], F32, name="radius")
             nc.gpsimd.tensor_tensor(out=radius[n][:], in0=sumsq[n][:], in1=half[:], op=ALU.pow)
 
+        def columns(n):
+            b, q = divmod(n, PAIRS)
+            return b, slice(PAIR * q, PAIR * (q + 1))
+
         def exponentials(n):
-            e_pos[n] = small.tile([P, PAIR], F32, name="e_pos")
-            e_neg[n] = small.tile([P, PAIR], F32, name="e_neg")
-            nc.scalar.activation(out=e_pos[n][:], in_=radius[n][:], func=ACT.Exp, bias=minus_ln2[:])
-            nc.scalar.activation(out=e_neg[n][:], in_=radius[n][:], func=ACT.Exp, bias=minus_ln2[:], scale=-1.0)
+            b, cols = columns(n)
+            if cols.start == 0:
+                e_pos[b] = small.tile([P, TILES], F32, name="e_pos")
+                e_neg[b] = small.tile([P, TILES], F32, name="e_neg")
+            nc.scalar.activation(out=e_pos[b][:, cols], in_=radius[n][:], func=ACT.Exp, bias=minus_ln2[:])
+            nc.scalar.activation(out=e_neg[b][:, cols], in_=radius[n][:], func=ACT.Exp, bias=minus_ln2[:], scale=-1.0)
 
         def invert(n):
             inverse[n] = small.tile([P, PAIR], F32, name="inverse")
             nc.vector.reciprocal(out=inverse[n][:], in_=radius[n][:])
 
         def subtract(n):
+            b, cols = columns(n)
             sinh[n] = small.tile([P, PAIR], F32, name="sinh")
-            nc.vector.tensor_sub(out=sinh[n][:], in0=e_pos[n][:], in1=e_neg[n][:])
+            nc.vector.tensor_sub(out=sinh[n][:], in0=e_pos[b][:, cols], in1=e_neg[b][:, cols])
+
+        def pairs_in_store(b):
+            return {GRAPHS - 1: 1, GRAPHS - 2: PAIRS // 2}.get(b, PAIRS)
 
         def take_cosh(n):
             b, q = divmod(n, PAIRS)
             if q == 0:
                 out_sb[b] = out_pool.tile([P, TILES, OUT_COLS], F32, name="out_sb")
-            nc.vector.tensor_add(out=out_sb[b][:, PAIR * q : PAIR * (q + 1), 0], in0=e_pos[n][:], in1=e_neg[n][:])
+            count = pairs_in_store(b)
+            if (q + 1) % count == 0:
+                rows = slice(PAIR * (q + 1 - count), PAIR * (q + 1))
+                nc.vector.tensor_add(out=out_sb[b][:, rows, 0], in0=e_pos[b][:, rows], in1=e_neg[b][:, rows])
 
         def scale_pair(n):
             b, q = divmod(n, PAIRS)
@@ -188,9 +204,10 @@ def tile_hgcn_pb_t_kernel(tc, x, w_sp, out):
         def store_after_pair(n):
             b, q = divmod(n, PAIRS)
             last_pair = q == PAIRS - 1
-            if b < GRAPHS - 1 and not last_pair:
+            count = pairs_in_store(b)
+            if (q + 1) % count:
                 return
-            first = PIECE * q if b == GRAPHS - 1 else 0
+            first = PIECE * (q + 1 - count)
             end = TILES * OUT_COLS if last_pair else PIECE * (q + 1)
             nc.scalar.dma_start(
                 out=out[b].rearrange("(p j) d -> p (j d)", j=TILES)[:, first:end],

@@ -27,7 +27,7 @@ OUT_COLS = 1 + DIMS
 RUN = 4
 LN2 = math.log(2.0)
 NUDGE = 2.0**-50
-PIECE = 1024
+PIECE = 512
 PAIRS_IN_PSUM = 3
 VECTOR_COPIES_EVERY = 2
 
@@ -35,6 +35,7 @@ MULTIPLY_AT = 2
 EXP_AT = 3
 SCALE_AT = 4
 STORE_AT = 5
+SYNC_STORES_FROM = GRAPHS - 2
 
 FLOPS = 2 * GRAPHS * NODES * FEATURES * DIMS
 
@@ -145,98 +146,117 @@ def tile_hgcn_pb_t_kernel(tc, x, w_sp, out):
                     )
 
         def sum_squares(n, i):
-            if i == 0:
-                sumsq[n] = small.tile([P, PAIR], F32, name="sumsq")
+            b, q = divmod(n, PAIRS)
+            if q == 0 and i == 0:
+                for kind, name in ((sumsq, "sumsq"), (radius, "radius"), (e_pos, "e_pos"), (e_neg, "e_neg"), (inverse, "inverse"), (sinh, "sinh")):
+                    kind[b] = small.tile([P, TILES], F32, name=name)
+                out_sb[b] = out_pool.tile([P, TILES, OUT_COLS], F32, name="out_sb")
+            j = PAIR * q + i
             squares = small.tile([P, DIMS], BF16, name="squares")
             nc.scalar.activation(
-                out=squares[:], in_=us[n, i][:], func=ACT.Square, bias=nudge[:], accum_out=sumsq[n][:, i : i + 1]
+                out=squares[:], in_=us[n, i][:], func=ACT.Square, bias=nudge[:], accum_out=sumsq[b][:, j : j + 1]
             )
 
-        def take_root(n):
-            radius[n] = small.tile([P, PAIR], F32, name="radius")
-            nc.gpsimd.tensor_tensor(out=radius[n][:], in0=sumsq[n][:], in1=half[:], op=ALU.pow)
+        def take_root(b, j, count):
+            cols = slice(j, j + count)
+            nc.gpsimd.tensor_tensor(out=radius[b][:, cols], in0=sumsq[b][:, cols], in1=half[:, :count], op=ALU.pow)
 
-        def columns(n):
-            b, q = divmod(n, PAIRS)
-            return b, slice(PAIR * q, PAIR * (q + 1))
+        def exponentials(b, j, count):
+            cols = slice(j, j + count)
+            nc.scalar.activation(out=e_pos[b][:, cols], in_=radius[b][:, cols], func=ACT.Exp, bias=minus_ln2[:])
+            nc.scalar.activation(
+                out=e_neg[b][:, cols], in_=radius[b][:, cols], func=ACT.Exp, bias=minus_ln2[:], scale=-1.0
+            )
 
-        def exponentials(n):
-            b, cols = columns(n)
-            if cols.start == 0:
-                e_pos[b] = small.tile([P, TILES], F32, name="e_pos")
-                e_neg[b] = small.tile([P, TILES], F32, name="e_neg")
-            nc.scalar.activation(out=e_pos[b][:, cols], in_=radius[n][:], func=ACT.Exp, bias=minus_ln2[:])
-            nc.scalar.activation(out=e_neg[b][:, cols], in_=radius[n][:], func=ACT.Exp, bias=minus_ln2[:], scale=-1.0)
+        def invert(b, j, count):
+            cols = slice(j, j + count)
+            nc.vector.reciprocal(out=inverse[b][:, cols], in_=radius[b][:, cols])
 
-        def invert(n):
-            inverse[n] = small.tile([P, PAIR], F32, name="inverse")
-            nc.vector.reciprocal(out=inverse[n][:], in_=radius[n][:])
+        def subtract(b, j, count):
+            cols = slice(j, j + count)
+            nc.vector.tensor_sub(out=sinh[b][:, cols], in0=e_pos[b][:, cols], in1=e_neg[b][:, cols])
 
-        def subtract(n):
-            b, cols = columns(n)
-            sinh[n] = small.tile([P, PAIR], F32, name="sinh")
-            nc.vector.tensor_sub(out=sinh[n][:], in0=e_pos[b][:, cols], in1=e_neg[b][:, cols])
+        def take_cosh(b, j, count):
+            rows = slice(j, j + count)
+            nc.vector.tensor_add(out=out_sb[b][:, rows, 0], in0=e_pos[b][:, rows], in1=e_neg[b][:, rows])
 
-        def pairs_in_store(b):
-            return {GRAPHS - 1: 1, GRAPHS - 2: PAIRS // 2}.get(b, PAIRS)
+        def scale_tile(b, j):
+            nc.vector.tensor_scalar(
+                out=out_sb[b][:, j, 1:],
+                in0=us[b * PAIRS + j // PAIR, j % PAIR][:],
+                scalar1=inverse[b][:, j : j + 1],
+                scalar2=sinh[b][:, j : j + 1],
+                op0=ALU.mult,
+                op1=ALU.mult,
+            )
 
-        def take_cosh(n):
-            b, q = divmod(n, PAIRS)
-            if q == 0:
-                out_sb[b] = out_pool.tile([P, TILES, OUT_COLS], F32, name="out_sb")
-            count = pairs_in_store(b)
-            if (q + 1) % count == 0:
-                rows = slice(PAIR * (q + 1 - count), PAIR * (q + 1))
-                nc.vector.tensor_add(out=out_sb[b][:, rows, 0], in0=e_pos[b][:, rows], in1=e_neg[b][:, rows])
-
-        def scale_pair(n):
-            b, q = divmod(n, PAIRS)
-            for i in range(PAIR):
-                nc.vector.tensor_scalar(
-                    out=out_sb[b][:, PAIR * q + i, 1:],
-                    in0=us[n, i][:],
-                    scalar1=inverse[n][:, i : i + 1],
-                    scalar2=sinh[n][:, i : i + 1],
-                    op0=ALU.mult,
-                    op1=ALU.mult,
-                )
-
-        def store_after_pair(n):
-            b, q = divmod(n, PAIRS)
-            last_pair = q == PAIRS - 1
-            count = pairs_in_store(b)
-            if (q + 1) % count:
-                return
-            first = PIECE * (q + 1 - count)
-            end = TILES * OUT_COLS if last_pair else PIECE * (q + 1)
-            nc.scalar.dma_start(
+        def store(b, j, count):
+            first = PIECE * j
+            end = TILES * OUT_COLS if j + count == TILES else PIECE * (j + count)
+            queue = nc.sync if b >= SYNC_STORES_FROM else nc.scalar
+            queue.dma_start(
                 out=out[b].rearrange("(p j) d -> p (j d)", j=TILES)[:, first:end],
                 in_=out_sb[b][:].rearrange("p j d -> p (j d)")[:, first:end],
             )
 
+        def pairs_in_store(b):
+            return {GRAPHS - 1: 1, GRAPHS - 2: PAIRS // 2}.get(b, PAIRS)
+
+        def stored_with(n):
+            b, q = divmod(n, PAIRS)
+            count = pairs_in_store(b)
+            return (b, PAIR * (q + 1 - count), PAIR * count) if (q + 1) % count == 0 else None
+
         def live(n):
             return 0 <= n < N_PAIRS
 
+        last = N_PAIRS - 1
         for s in range(N_PAIRS + STORE_AT):
             if live(s):
                 transpose_pair(s)
                 copy_out_pair(s)
-            if live(s - MULTIPLY_AT):
-                multiply_pair(s - MULTIPLY_AT)
-            if live(s - SCALE_AT):
-                scale_pair(s - SCALE_AT)
-            if live(s - MULTIPLY_AT):
-                sum_squares(s - MULTIPLY_AT, 0)
-            if live(s - STORE_AT):
-                store_after_pair(s - STORE_AT)
-            if live(s - EXP_AT):
-                invert(s - EXP_AT)
-                exponentials(s - EXP_AT)
-                subtract(s - EXP_AT)
-            if live(s - MULTIPLY_AT):
-                sum_squares(s - MULTIPLY_AT, 1)
-                take_root(s - MULTIPLY_AT)
+            n = s - MULTIPLY_AT
+            if live(n):
+                multiply_pair(n)
+            n = s - SCALE_AT
+            if live(n) and n != last:
+                b, q = divmod(n, PAIRS)
+                for i in range(PAIR):
+                    scale_tile(b, PAIR * q + i)
+                if b >= SYNC_STORES_FROM and stored_with(n):
+                    store(*stored_with(n))
+            n = s - MULTIPLY_AT
+            if live(n):
+                sum_squares(n, 0)
+                if n == last:
+                    take_root(GRAPHS - 1, TILES - PAIR, 1)
+            n = s - STORE_AT
+            if live(n) and n // PAIRS < SYNC_STORES_FROM and stored_with(n):
+                store(*stored_with(n))
+            n = s - EXP_AT
+            if live(n) and n != last:
+                b, q = divmod(n, PAIRS)
+                invert(b, PAIR * q, PAIR)
+                exponentials(b, PAIR * q, PAIR)
+                subtract(b, PAIR * q, PAIR)
+            if n == last:
+                for j in range(TILES - PAIR, TILES):
+                    exponentials(GRAPHS - 1, j, 1)
+                    invert(GRAPHS - 1, j, 1)
+                    subtract(GRAPHS - 1, j, 1)
+                    take_cosh(GRAPHS - 1, j, 1)
+                    scale_tile(GRAPHS - 1, j)
+                    store(GRAPHS - 1, j, 1)
+            n = s - MULTIPLY_AT
+            if live(n):
+                b, q = divmod(n, PAIRS)
+                sum_squares(n, 1)
+                if n == last:
+                    take_root(GRAPHS - 1, TILES - 1, 1)
+                else:
+                    take_root(b, PAIR * q, PAIR)
             if live(s):
                 quantise_pair(s)
-            if live(s - EXP_AT):
-                take_cosh(s - EXP_AT)
+            n = s - EXP_AT
+            if live(n) and n != last and stored_with(n):
+                take_cosh(*stored_with(n))

@@ -29,7 +29,7 @@ LN2 = math.log(2.0)
 NUDGE = 2.0**-50
 PIECE = 512
 PAIRS_IN_PSUM = 3
-VECTOR_COPIES_EVERY = 2
+FIRST_SHARED_PAIR = 1
 
 MULTIPLY_AT = 2
 EXP_AT = 3
@@ -119,8 +119,9 @@ def tile_hgcn_pb_t_kernel(tc, x, w_sp, out):
                 dst = grouped[n][:, i * TILE_COLS : (i + 1) * TILE_COLS].bitcast(F32)
                 dst = dst.rearrange("p (g r u) -> p g r u", g=PASSES, u=HALVES)
                 src = x_t[n, i][:].rearrange("p g u r -> p g r u")
-                if i == PAIR - 1 and n % VECTOR_COPIES_EVERY == VECTOR_COPIES_EVERY - 1:
-                    nc.vector.tensor_copy(out=dst, in_=src)
+                if i == 0 and n >= FIRST_SHARED_PAIR:
+                    nc.scalar.copy(out=dst[:, 0], in_=src[:, 0])
+                    nc.vector.tensor_copy(out=dst[:, 1], in_=src[:, 1])
                 else:
                     nc.scalar.copy(out=dst, in_=src)
 

@@ -34,8 +34,7 @@ FIRST_SHARED_PAIR = 1
 MULTIPLY_AT = 2
 EXP_AT = 3
 SCALE_AT = 4
-STORE_AT = 5
-SYNC_STORES_FROM = GRAPHS - 2
+LOADED_AHEAD = 5
 
 FLOPS = 2 * GRAPHS * NODES * FEATURES * DIMS
 
@@ -74,7 +73,7 @@ def tile_hgcn_pb_t_kernel(tc, x, w_sp, out):
             load_nodes(0, PAIR * q, PAIR)
         for j in range(0, TILES, TILES // 2):
             load_nodes(1, j, TILES // 2)
-        for b in range(2, GRAPHS):
+        for b in range(2, LOADED_AHEAD):
             load_nodes(b, 0, TILES)
 
         ident = const.tile([P, P], F32)
@@ -194,8 +193,7 @@ def tile_hgcn_pb_t_kernel(tc, x, w_sp, out):
         def store(b, j, count):
             first = PIECE * j
             end = TILES * OUT_COLS if j + count == TILES else PIECE * (j + count)
-            queue = nc.sync if b >= SYNC_STORES_FROM else nc.scalar
-            queue.dma_start(
+            nc.sync.dma_start(
                 out=out[b].rearrange("(p j) d -> p (j d)", j=TILES)[:, first:end],
                 in_=out_sb[b][:].rearrange("p j d -> p (j d)")[:, first:end],
             )
@@ -212,7 +210,7 @@ def tile_hgcn_pb_t_kernel(tc, x, w_sp, out):
             return 0 <= n < N_PAIRS
 
         last = N_PAIRS - 1
-        for s in range(N_PAIRS + STORE_AT):
+        for s in range(N_PAIRS + SCALE_AT):
             if live(s):
                 transpose_pair(s)
                 copy_out_pair(s)
@@ -224,16 +222,15 @@ def tile_hgcn_pb_t_kernel(tc, x, w_sp, out):
                 b, q = divmod(n, PAIRS)
                 for i in range(PAIR):
                     scale_tile(b, PAIR * q + i)
-                if b >= SYNC_STORES_FROM and stored_with(n):
+                if stored_with(n):
                     store(*stored_with(n))
+                    if b + LOADED_AHEAD < GRAPHS:
+                        load_nodes(b + LOADED_AHEAD, 0, TILES)
             n = s - MULTIPLY_AT
             if live(n):
                 sum_squares(n, 0)
                 if n == last:
                     take_root(GRAPHS - 1, TILES - PAIR, 1)
-            n = s - STORE_AT
-            if live(n) and n // PAIRS < SYNC_STORES_FROM and stored_with(n):
-                store(*stored_with(n))
             n = s - EXP_AT
             if live(n) and n != last:
                 b, q = divmod(n, PAIRS)

@@ -29,6 +29,8 @@ LN2 = math.log(2.0)
 NUDGE = 2.0**-50
 PIECE = 512
 PAIRS_IN_PSUM = 3
+VECTOR_RUNS = 80
+LATE_PAIRS = 2
 FIRST_SHARED_PAIR = 1
 
 MULTIPLY_AT = 2
@@ -90,10 +92,12 @@ def tile_hgcn_pb_t_kernel(tc, x, w_sp, out):
         w_codes = const.tile([P, PASSES * DIMS], U32, align_bytes=64)
         w_scales = const.tile([P, PASSES * DIMS], U8, align_bytes=64)
         for g in range(PASSES):
-            nc.vector.tensor_copy(
-                out=w_grouped[:, g].rearrange("p (c i) t -> p c t i", i=RUN),
-                in_=w_raw[:, g].rearrange("p t (c i) -> p c t i", i=RUN),
-            )
+            grouped_view = w_grouped[:, g].rearrange("p (c i) t -> p c t i", i=RUN)
+            raw_view = w_raw[:, g].rearrange("p t (c i) -> p c t i", i=RUN)
+            cut = DIMS // RUN if g == 0 else VECTOR_RUNS
+            nc.vector.tensor_copy(out=grouped_view[:, :cut], in_=raw_view[:, :cut])
+            if cut < DIMS // RUN:
+                nc.scalar.copy(out=grouped_view[:, cut:], in_=raw_view[:, cut:])
             dims = slice(g * DIMS, (g + 1) * DIMS)
             nc.vector.quantize_mx(
                 out=w_codes[:, dims].bitcast(FP8X4),
@@ -131,12 +135,17 @@ def tile_hgcn_pb_t_kernel(tc, x, w_sp, out):
 
         def multiply_pair(n):
             for i in range(PAIR):
-                us[n, i] = us_pool.tile([P, DIMS], F32, name="us")
+                if n == N_PAIRS - LATE_PAIRS:
+                    bank = xt_pool.tile([P, PASSES, HALVES, P], F32, name="x_t")
+                    us[n, i] = bank[:].rearrange("p g u r -> p (g u r)")
+                else:
+                    bank = us_pool.tile([P, DIMS], F32, name="us")
+                    us[n, i] = bank[:]
                 for g in range(PASSES):
                     nodes = slice((i * PASSES + g) * P, (i * PASSES + g + 1) * P)
                     dims = slice(g * DIMS, (g + 1) * DIMS)
                     nc.tensor.matmul_mx(
-                        out=us[n, i][:],
+                        out=us[n, i],
                         lhsT=codes[n][:, nodes].bitcast(FP8X4),
                         lhsT_scale=scales[n][:, nodes],
                         rhs=w_codes[:, dims].bitcast(FP8X4),
@@ -154,7 +163,7 @@ def tile_hgcn_pb_t_kernel(tc, x, w_sp, out):
             j = PAIR * q + i
             squares = small.tile([P, DIMS], BF16, name="squares")
             nc.scalar.activation(
-                out=squares[:], in_=us[n, i][:], func=ACT.Square, bias=nudge[:], accum_out=sumsq[b][:, j : j + 1]
+                out=squares[:], in_=us[n, i], func=ACT.Square, bias=nudge[:], accum_out=sumsq[b][:, j : j + 1]
             )
 
         def take_root(b, j, count):
@@ -183,7 +192,7 @@ def tile_hgcn_pb_t_kernel(tc, x, w_sp, out):
         def scale_tile(b, j):
             nc.vector.tensor_scalar(
                 out=out_sb[b][:, j, 1:],
-                in0=us[b * PAIRS + j // PAIR, j % PAIR][:],
+                in0=us[b * PAIRS + j // PAIR, j % PAIR],
                 scalar1=inverse[b][:, j : j + 1],
                 scalar2=sinh[b][:, j : j + 1],
                 op0=ALU.mult,
@@ -210,6 +219,15 @@ def tile_hgcn_pb_t_kernel(tc, x, w_sp, out):
             return 0 <= n < N_PAIRS
 
         last = N_PAIRS - 1
+
+        def finish_squares(n):
+            b, q = divmod(n, PAIRS)
+            sum_squares(n, 1)
+            if n == last:
+                take_root(b, TILES - 1, 1)
+            else:
+                take_root(b, PAIR * q, PAIR)
+
         for s in range(N_PAIRS + SCALE_AT):
             if live(s):
                 transpose_pair(s)
@@ -220,17 +238,22 @@ def tile_hgcn_pb_t_kernel(tc, x, w_sp, out):
             n = s - SCALE_AT
             if live(n) and n != last:
                 b, q = divmod(n, PAIRS)
-                for i in range(PAIR):
-                    scale_tile(b, PAIR * q + i)
+                scale_tile(b, PAIR * q)
+                if stored_with(n):
+                    take_cosh(*stored_with(n))
+                scale_tile(b, PAIR * q + 1)
                 if stored_with(n):
                     store(*stored_with(n))
                     if b + LOADED_AHEAD < GRAPHS:
                         load_nodes(b + LOADED_AHEAD, 0, TILES)
             n = s - MULTIPLY_AT
+            late = n >= N_PAIRS - LATE_PAIRS
             if live(n):
                 sum_squares(n, 0)
                 if n == last:
                     take_root(GRAPHS - 1, TILES - PAIR, 1)
+                if late:
+                    finish_squares(n)
             n = s - EXP_AT
             if live(n) and n != last:
                 b, q = divmod(n, PAIRS)
@@ -246,15 +269,7 @@ def tile_hgcn_pb_t_kernel(tc, x, w_sp, out):
                     scale_tile(GRAPHS - 1, j)
                     store(GRAPHS - 1, j, 1)
             n = s - MULTIPLY_AT
-            if live(n):
-                b, q = divmod(n, PAIRS)
-                sum_squares(n, 1)
-                if n == last:
-                    take_root(GRAPHS - 1, TILES - 1, 1)
-                else:
-                    take_root(b, PAIR * q, PAIR)
+            if live(n) and not late:
+                finish_squares(n)
             if live(s):
                 quantise_pair(s)
-            n = s - EXP_AT
-            if live(n) and n != last and stored_with(n):
-                take_cosh(*stored_with(n))

@@ -31,7 +31,8 @@ PIECE = 512
 PAIRS_IN_PSUM = 3
 VECTOR_RUNS = 80
 LATE_PAIRS = 2
-FIRST_SHARED_PAIR = 1
+BUSY_AT_START = 8
+FIRST_SHARED_PAIR = 2
 
 MULTIPLY_AT = 2
 EXP_AT = 3
@@ -69,15 +70,16 @@ def tile_hgcn_pb_t_kernel(tc, x, w_sp, out):
         w_rows = w_sp.rearrange("(g u p e) d -> g p u (e d)", g=PASSES, u=HALVES, p=P)
         for g in range(PASSES):
             nc.sync.dma_start(out=w_raw[:, g].rearrange("p (u e) d -> p u (e d)", u=HALVES), in_=w_rows[g])
-        for j in range(PAIR):
+        for j in range(TILES - PAIR):
             load_nodes(0, j, 1)
-        for q in range(1, PAIRS):
-            load_nodes(0, PAIR * q, PAIR)
+        load_nodes(0, TILES - PAIR, PAIR)
         for j in range(0, TILES, TILES // 2):
             load_nodes(1, j, TILES // 2)
         for b in range(2, LOADED_AHEAD):
             load_nodes(b, 0, TILES)
 
+        zeros = const.tile([P, DIMS], BF16)
+        nc.vector.memset(zeros[:], 0.0)
         ident = const.tile([P, P], F32)
         make_identity(nc, ident[:])
         half = const.tile([P, PAIR], F32)
@@ -87,6 +89,14 @@ def tile_hgcn_pb_t_kernel(tc, x, w_sp, out):
         minus_ln2 = const.tile([P, 1], F32)
         nc.gpsimd.memset(minus_ln2[:], 1.0)
         nc.vector.tensor_scalar(out=minus_ln2[:], in0=minus_ln2[:], scalar1=-LN2, scalar2=None, op0=ALU.mult)
+
+        idle_bank = us_pool.tile([P, DIMS], F32, name="us")
+
+        def keep_busy():
+            nc.tensor.matmul(idle_bank[:], lhsT=zeros[:, :P], rhs=zeros[:], start=True, stop=True)
+
+        for i in range(BUSY_AT_START):
+            keep_busy()
 
         w_grouped = const.tile([P, PASSES, DIMS, PACK], BF16, align_bytes=64)
         w_codes = const.tile([P, PASSES * DIMS], U32, align_bytes=64)
@@ -115,6 +125,8 @@ def tile_hgcn_pb_t_kernel(tc, x, w_sp, out):
                         first = (g * HALVES + u) * P
                         nc.tensor.transpose(bank[:, g, u, :], words[:, first : first + P], ident[:])
                 x_t[n, i] = bank
+                if n < MULTIPLY_AT:
+                    keep_busy()
 
         def copy_out_pair(n):
             grouped[n] = mx_pool.tile([P, PAIR * TILE_COLS], BF16, align_bytes=64, name="grouped")
@@ -189,10 +201,10 @@ def tile_hgcn_pb_t_kernel(tc, x, w_sp, out):
             rows = slice(j, j + count)
             nc.vector.tensor_add(out=out_sb[b][:, rows, 0], in0=e_pos[b][:, rows], in1=e_neg[b][:, rows])
 
-        def scale_tile(b, j):
+        def scale_tile(b, j, dims=slice(0, DIMS)):
             nc.vector.tensor_scalar(
-                out=out_sb[b][:, j, 1:],
-                in0=us[b * PAIRS + j // PAIR, j % PAIR],
+                out=out_sb[b][:, j, 1 + dims.start : 1 + dims.stop],
+                in0=us[b * PAIRS + j // PAIR, j % PAIR][:, dims],
                 scalar1=inverse[b][:, j : j + 1],
                 scalar2=sinh[b][:, j : j + 1],
                 op0=ALU.mult,
@@ -200,8 +212,9 @@ def tile_hgcn_pb_t_kernel(tc, x, w_sp, out):
             )
 
         def store(b, j, count):
-            first = PIECE * j
-            end = TILES * OUT_COLS if j + count == TILES else PIECE * (j + count)
+            store_words(b, PIECE * j, TILES * OUT_COLS if j + count == TILES else PIECE * (j + count))
+
+        def store_words(b, first, end):
             nc.sync.dma_start(
                 out=out[b].rearrange("(p j) d -> p (j d)", j=TILES)[:, first:end],
                 in_=out_sb[b][:].rearrange("p j d -> p (j d)")[:, first:end],
@@ -266,8 +279,14 @@ def tile_hgcn_pb_t_kernel(tc, x, w_sp, out):
                     invert(GRAPHS - 1, j, 1)
                     subtract(GRAPHS - 1, j, 1)
                     take_cosh(GRAPHS - 1, j, 1)
-                    scale_tile(GRAPHS - 1, j)
-                    store(GRAPHS - 1, j, 1)
+                    if j < TILES - 1:
+                        scale_tile(GRAPHS - 1, j)
+                        store(GRAPHS - 1, j, 1)
+                middle = OUT_COLS * (TILES - 1) + 1 + DIMS // 2
+                scale_tile(GRAPHS - 1, TILES - 1, slice(0, DIMS // 2))
+                store_words(GRAPHS - 1, PIECE * (TILES - 1), middle)
+                scale_tile(GRAPHS - 1, TILES - 1, slice(DIMS // 2, DIMS))
+                store_words(GRAPHS - 1, middle, TILES * OUT_COLS)
             n = s - MULTIPLY_AT
             if live(n) and not late:
                 finish_squares(n)

import math

import concourse.mybir as mybir
from concourse.masks import make_identity

BF16 = mybir.dt.bfloat16
F32 = mybir.dt.float32
U32 = mybir.dt.uint32
U8 = mybir.dt.uint8
FP8X4 = mybir.dt.float8_e4m3fn_x4
ACT = mybir.ActivationFunctionType
ALU = mybir.AluOpType

P = 128
GRAPHS, NODES, FEATURES, DIMS = 8, 1024, 1024, 512
PACK = 4
K_PASS = P * PACK
PASSES = FEATURES // K_PASS
HALVES = 2
TILES = NODES // P
PAIR = 2
PAIRS = TILES // PAIR
N_PAIRS = GRAPHS * PAIRS
TILE_COLS = PASSES * P * PACK
TILE_WORDS = PASSES * P
OUT_COLS = 1 + DIMS
RUN = 4
LN2 = math.log(2.0)
NUDGE = 2.0**-50
PIECE = 512
PAIRS_IN_PSUM = 3
VECTOR_RUNS = 80
LATE_PAIRS = 2
BUSY_AT_START = 8
FIRST_SHARED_PAIR = 2

MULTIPLY_AT = 2
EXP_AT = 3
SCALE_AT = 4
LOADED_AHEAD = 5

FLOPS = 2 * GRAPHS * NODES * FEATURES * DIMS


def tile_hgcn_pb_t_kernel(tc, x, w_sp, out):
    nc = tc.nc
    with (
        tc.tile_pool(name="const", bufs=1) as const,
        tc.tile_pool(name="x_pool", bufs=GRAPHS) as x_pool,
        tc.tile_pool(name="out_pool", bufs=3) as out_pool,
        tc.tile_pool(name="mx_pool", bufs=MULTIPLY_AT + 2) as mx_pool,
        tc.tile_pool(name="small", bufs=4) as small,
        tc.psum_pool(name="xt_pool", bufs=PAIR) as xt_pool,
        tc.psum_pool(name="us_pool", bufs=PAIRS_IN_PSUM * PAIR) as us_pool,
        tc.manual_schedule(),
    ):
        x_sb, out_sb = {}, {}
        x_t, grouped, codes, scales, us = {}, {}, {}, {}, {}
        sumsq, radius, e_pos, e_neg, inverse, sinh = {}, {}, {}, {}, {}, {}

        def load_nodes(b, first_tile, n_tiles):
            rows = x[b].rearrange("(p j) k -> p j k", j=TILES)
            cut = slice(first_tile, first_tile + n_tiles)
            nc.sync.dma_start(out=x_sb[b][:, cut, :], in_=rows[:, cut, :])

        for b in range(GRAPHS):
            x_sb[b] = x_pool.tile([P, TILES, FEATURES], BF16, name="x_sb")

        w_raw = const.tile([P, PASSES, PACK, DIMS], BF16)
        w_rows = w_sp.rearrange("(g u p e) d -> g p u (e d)", g=PASSES, u=HALVES, p=P)
        for g in range(PASSES):
            nc.sync.dma_start(out=w_raw[:, g].rearrange("p (u e) d -> p u (e d)", u=HALVES), in_=w_rows[g])
        for j in range(TILES - PAIR):
            load_nodes(0, j, 1)
        load_nodes(0, TILES - PAIR, PAIR)
        for j in range(0, TILES, TILES // 2):
            load_nodes(1, j, TILES // 2)
        for b in range(2, LOADED_AHEAD):
            load_nodes(b, 0, TILES)

        zeros = const.tile([P, DIMS], BF16)
        nc.vector.memset(zeros[:], 0.0)
        ident = const.tile([P, P], F32)
        make_identity(nc, ident[:])
        half = const.tile([P, PAIR], F32)
        nc.gpsimd.memset(half[:], 0.5)
        nudge = const.tile([P, 1], F32)
        nc.gpsimd.memset(nudge[:], NUDGE)
        minus_ln2 = const.tile([P, 1], F32)
        nc.gpsimd.memset(minus_ln2[:], 1.0)
        nc.vector.tensor_scalar(out=minus_ln2[:], in0=minus_ln2[:], scalar1=-LN2, scalar2=None, op0=ALU.mult)

        idle_bank = us_pool.tile([P, DIMS], F32, name="us")

        def keep_busy():
            nc.tensor.matmul(idle_bank[:], lhsT=zeros[:, :P], rhs=zeros[:], start=True, stop=True)

        for i in range(BUSY_AT_START):
            keep_busy()

        w_grouped = const.tile([P, PASSES, DIMS, PACK], BF16, align_bytes=64)
        w_codes = const.tile([P, PASSES * DIMS], U32, align_bytes=64)
        w_scales = const.tile([P, PASSES * DIMS], U8, align_bytes=64)
        for g in range(PASSES):
            grouped_view = w_grouped[:, g].rearrange("p (c i) t -> p c t i", i=RUN)
            raw_view = w_raw[:, g].rearrange("p t (c i) -> p c t i", i=RUN)
            cut = DIMS // RUN if g == 0 else VECTOR_RUNS
            nc.vector.tensor_copy(out=grouped_view[:, :cut], in_=raw_view[:, :cut])
            if cut < DIMS // RUN:
                nc.scalar.copy(out=grouped_view[:, cut:], in_=raw_view[:, cut:])
            dims = slice(g * DIMS, (g + 1) * DIMS)
            nc.vector.quantize_mx(
                out=w_codes[:, dims].bitcast(FP8X4),
                scales=w_scales[:, dims],
                in_=w_grouped[:, g].rearrange("p d t -> p (d t)"),
            )

        def transpose_pair(n):
            b, q = divmod(n, PAIRS)
            for i in range(PAIR):
                words = x_sb[b][:, PAIR * q + i, :].bitcast(F32)
                bank = xt_pool.tile([P, PASSES, HALVES, P], F32, name="x_t")
                for g in range(PASSES):
                    for u in range(HALVES):
                        first = (g * HALVES + u) * P
                        nc.tensor.transpose(bank[:, g, u, :], words[:, first : first + P], ident[:])
                x_t[n, i] = bank
                if n < MULTIPLY_AT:
                    keep_busy()

        def copy_out_pair(n):
            grouped[n] = mx_pool.tile([P, PAIR * TILE_COLS], BF16, align_bytes=64, name="grouped")
            for i in range(PAIR):
                dst = grouped[n][:, i * TILE_COLS : (i + 1) * TILE_COLS].bitcast(F32)
                dst = dst.rearrange("p (g r u) -> p g r u", g=PASSES, u=HALVES)
                src = x_t[n, i][:].rearrange("p g u r -> p g r u")
                if i == 0 and n >= FIRST_SHARED_PAIR:
                    nc.scalar.copy(out=dst[:, 0], in_=src[:, 0])
                    nc.vector.tensor_copy(out=dst[:, 1], in_=src[:, 1])
                else:
                    nc.scalar.copy(out=dst, in_=src)

        def quantise_pair(n):
            codes[n] = mx_pool.tile([P, PAIR * TILE_WORDS], U32, align_bytes=64, name="codes")
            scales[n] = mx_pool.tile([P, PAIR * TILE_WORDS], U8, align_bytes=64, name="scales")
            nc.vector.quantize_mx(out=codes[n][:].bitcast(FP8X4), scales=scales[n][:], in_=grouped[n][:])

        def multiply_pair(n):
            for i in range(PAIR):
                if n == N_PAIRS - LATE_PAIRS:
                    bank = xt_pool.tile([P, PASSES, HALVES, P], F32, name="x_t")
                    us[n, i] = bank[:].rearrange("p g u r -> p (g u r)")
                else:
                    bank = us_pool.tile([P, DIMS], F32, name="us")
                    us[n, i] = bank[:]
                for g in range(PASSES):
                    nodes = slice((i * PASSES + g) * P, (i * PASSES + g + 1) * P)
                    dims = slice(g * DIMS, (g + 1) * DIMS)
                    nc.tensor.matmul_mx(
                        out=us[n, i],
                        lhsT=codes[n][:, nodes].bitcast(FP8X4),
                        lhsT_scale=scales[n][:, nodes],
                        rhs=w_codes[:, dims].bitcast(FP8X4),
                        rhs_scale=w_scales[:, dims],
                        start=(g == 0),
                        stop=(g == PASSES - 1),
                    )

        def sum_squares(n, i):
            b, q = divmod(n, PAIRS)
            if q == 0 and i == 0:
                for kind, name in ((sumsq, "sumsq"), (radius, "radius"), (e_pos, "e_pos"), (e_neg, "e_neg"), (inverse, "inverse"), (sinh, "sinh")):
                    kind[b] = small.tile([P, TILES], F32, name=name)
                out_sb[b] = out_pool.tile([P, TILES, OUT_COLS], F32, name="out_sb")
            j = PAIR * q + i
            squares = small.tile([P, DIMS], BF16, name="squares")
            nc.scalar.activation(
                out=squares[:], in_=us[n, i], func=ACT.Square, bias=nudge[:], accum_out=sumsq[b][:, j : j + 1]
            )

        def take_root(b, j, count):
            cols = slice(j, j + count)
            nc.gpsimd.tensor_tensor(out=radius[b][:, cols], in0=sumsq[b][:, cols], in1=half[:, :count], op=ALU.pow)

        def exponentials(b, j, count):
            cols = slice(j, j + count)
            nc.scalar.activation(out=e_pos[b][:, cols], in_=radius[b][:, cols], func=ACT.Exp, bias=minus_ln2[:])
            nc.scalar.activation(
                out=e_neg[b][:, cols], in_=radius[b][:, cols], func=ACT.Exp, bias=minus_ln2[:], scale=-1.0
            )

        def invert(b, j, count):
            cols = slice(j, j + count)
            nc.vector.reciprocal(out=inverse[b][:, cols], in_=radius[b][:, cols])

        def subtract(b, j, count):
            cols = slice(j, j + count)
            nc.vector.tensor_sub(out=sinh[b][:, cols], in0=e_pos[b][:, cols], in1=e_neg[b][:, cols])

        def take_cosh(b, j, count):
            rows = slice(j, j + count)
            nc.vector.tensor_add(out=out_sb[b][:, rows, 0], in0=e_pos[b][:, rows], in1=e_neg[b][:, rows])

        def scale_tile(b, j, dims=slice(0, DIMS)):
            nc.vector.tensor_scalar(
                out=out_sb[b][:, j, 1 + dims.start : 1 + dims.stop],
                in0=us[b * PAIRS + j // PAIR, j % PAIR][:, dims],
                scalar1=inverse[b][:, j : j + 1],
                scalar2=sinh[b][:, j : j + 1],
                op0=ALU.mult,
                op1=ALU.mult,
            )

        def store(b, j, count):
            store_words(b, PIECE * j, TILES * OUT_COLS if j + count == TILES else PIECE * (j + count))

        def store_words(b, first, end):
            nc.sync.dma_start(
                out=out[b].rearrange("(p j) d -> p (j d)", j=TILES)[:, first:end],
                in_=out_sb[b][:].rearrange("p j d -> p (j d)")[:, first:end],
            )

        def pairs_in_store(b):
            return {GRAPHS - 1: 1, GRAPHS - 2: PAIRS // 2}.get(b, PAIRS)

        def stored_with(n):
            b, q = divmod(n, PAIRS)
            count = pairs_in_store(b)
            return (b, PAIR * (q + 1 - count), PAIR * count) if (q + 1) % count == 0 else None

        def live(n):
            return 0 <= n < N_PAIRS

        last = N_PAIRS - 1

        def finish_squares(n):
            b, q = divmod(n, PAIRS)
            sum_squares(n, 1)
            if n == last:
                take_root(b, TILES - 1, 1)
            else:
                take_root(b, PAIR * q, PAIR)

        for s in range(N_PAIRS + SCALE_AT):
            if live(s):
                transpose_pair(s)
                copy_out_pair(s)
            n = s - MULTIPLY_AT
            if live(n):
                multiply_pair(n)
            n = s - SCALE_AT
            if live(n) and n != last:
                b, q = divmod(n, PAIRS)
                scale_tile(b, PAIR * q)
                if stored_with(n):
                    take_cosh(*stored_with(n))
                scale_tile(b, PAIR * q + 1)
                if stored_with(n):
                    store(*stored_with(n))
                    if b + LOADED_AHEAD < GRAPHS:
                        load_nodes(b + LOADED_AHEAD, 0, TILES)
            n = s - MULTIPLY_AT
            late = n >= N_PAIRS - LATE_PAIRS
            if live(n):
                sum_squares(n, 0)
                if n == last:
                    take_root(GRAPHS - 1, TILES - PAIR, 1)
                if late:
                    finish_squares(n)
            n = s - EXP_AT
            if live(n) and n != last:
                b, q = divmod(n, PAIRS)
                invert(b, PAIR * q, PAIR)
                exponentials(b, PAIR * q, PAIR)
                subtract(b, PAIR * q, PAIR)
            if n == last:
                for j in range(TILES - PAIR, TILES):
                    exponentials(GRAPHS - 1, j, 1)
                    invert(GRAPHS - 1, j, 1)
                    subtract(GRAPHS - 1, j, 1)
                    take_cosh(GRAPHS - 1, j, 1)
                    if j < TILES - 1:
                        scale_tile(GRAPHS - 1, j)
                        store(GRAPHS - 1, j, 1)
                middle = OUT_COLS * (TILES - 1) + 1 + DIMS // 2
                scale_tile(GRAPHS - 1, TILES - 1, slice(0, DIMS // 2))
                store_words(GRAPHS - 1, PIECE * (TILES - 1), middle)
                scale_tile(GRAPHS - 1, TILES - 1, slice(DIMS // 2, DIMS))
                store_words(GRAPHS - 1, middle, TILES * OUT_COLS)
            n = s - MULTIPLY_AT
            if live(n) and not late:
                finish_squares(n)
            if live(s):
                quantise_pair(s)
